import numpy as np
import ml_dtypes


def mxq(x, axis, fmt="e4m3"):
    dtype, down = {"e4m3": (ml_dtypes.float8_e4m3fn, 7), "e5m2": (ml_dtypes.float8_e5m2, 14)}[fmt]
    v = np.moveaxis(np.asarray(x, np.float32).astype(ml_dtypes.bfloat16).astype(np.float64), axis, -1)
    blocks = v.reshape(v.shape[:-1] + (-1, 32))
    amax = np.abs(blocks).max(-1, keepdims=True)
    byte = np.maximum(np.where(amax > 0, np.frexp(amax)[1] - 1 + 127, 0) - down, 1)
    scale = np.exp2(byte - 127.0)
    codes = (blocks / scale).astype(np.float32).astype(dtype).astype(np.float64)
    return np.moveaxis((codes * scale).reshape(v.shape), -1, axis)


WIDE = False


def mx_kscale(k):
    if not WIDE:
        return np.ones(k)
    levels = np.array([10, -10, 5, -5, 0])
    a = np.random.permutation(np.resize(levels, k // 512 * 4)).reshape(k // 512, 4)
    idx = np.arange(k)
    return np.exp2(a[idx // 512, idx % 128 // 32])


BF16 = ml_dtypes.bfloat16


def bf(x):
    return np.asarray(x, np.float32).astype(BF16)


def f64(x):
    return np.asarray(x).astype(np.float64)


E2M1 = np.array([0.0, 0.5, 1.0, 1.5, 2.0, 3.0, 4.0, 6.0, -0.0, -0.5, -1.0, -1.5, -2.0, -3.0, -4.0, -6.0])


def pack_weight(w, fmt):
    k, n = w.shape
    w = f64(bf(w)).reshape(k // 32, 32, n)
    amax = np.abs(w).max(1)
    if fmt == "e4m3":
        byte = np.frexp(amax)[1] - 1 + 127 - 7
    else:
        mant, ex = np.frexp(amax / 6.0)
        byte = np.where(mant > 0.5, ex, ex - 1) + 127
    byte = np.clip(np.where(amax > 0, byte, 1), 1, 254)
    scaled = (w * np.exp2(127.0 - byte)[:, None, :]).reshape(k, n).astype(np.float32)
    by_word = np.ascontiguousarray(scaled.reshape(k // 512, 128, 4, n).transpose(0, 1, 3, 2))
    if fmt == "e4m3":
        words = by_word.astype(ml_dtypes.float8_e4m3fn).view(np.uint8)
    else:
        c = by_word.astype(ml_dtypes.float4_e2m1fn).view(np.uint8) & 0xF
        words = c[..., 0::2] | (c[..., 1::2] << 4)
    return np.ascontiguousarray(words), np.ascontiguousarray(byte.astype(np.uint8).reshape(k // 512, 16, n))


def unpack_weight(words, scales, fmt):
    g, p, n, _ = words.shape
    if fmt == "e4m3":
        vals = np.ascontiguousarray(words).view(ml_dtypes.float8_e4m3fn).astype(np.float64)
    else:
        nib = np.empty((g, p, n, 4), np.uint8)
        nib[..., 0::2] = words & 0xF
        nib[..., 1::2] = words >> 4
        vals = E2M1[nib]
    vals = vals * np.repeat(np.exp2(scales.astype(np.float64) - 127.0), 8, axis=1)[..., None]
    return vals.transpose(0, 1, 3, 2).reshape(g * 512, n)


N, DIN, DOUT = 128, 4096, 4096
C = 1.0
MIN_NORM = 1e-15
EPS_PROJ = 4e-3


def safe_norm(v):
    return np.sqrt(np.maximum(np.sum(v * v, axis=-1, keepdims=True), MIN_NORM))


def artanh(u):
    u = np.clip(u, -1.0 + 1e-5, 1.0 - 1e-5)
    return 0.5 * np.log((1.0 + u) / (1.0 - u))


def project(v, c):
    norm = safe_norm(v)
    maxnorm = (1.0 - EPS_PROJ) / np.sqrt(c)
    return np.where(norm > maxnorm, v / norm * maxnorm, v)


def mobius_matvec(W, x, c):
    sqc = np.sqrt(c)
    x_norm = safe_norm(x)
    mx = mxq(x, 1, "e4m3") @ W.T
    mx_norm = safe_norm(mx)
    res = np.tanh(mx_norm / x_norm * artanh(sqc * x_norm)) * mx / (mx_norm * sqc)
    zero = np.all(mx == 0, axis=-1, keepdims=True)
    return np.where(zero, 0.0, res)


def expmap0(u, c):
    sqc = np.sqrt(c)
    u_norm = safe_norm(u)
    return np.tanh(sqc * u_norm) * u / (sqc * u_norm)


def mobius_add(x, y, c):
    x2 = np.sum(x * x, axis=-1, keepdims=True)
    y2 = np.sum(y * y, axis=-1, keepdims=True)
    xy = np.sum(x * y, axis=-1, keepdims=True)
    num = (1.0 + 2.0 * c * xy + c * y2) * x + (1.0 - c * x2) * y
    denom = 1.0 + 2.0 * c * xy + c * c * x2 * y2
    return num / np.maximum(denom, MIN_NORM)


def setup_inputs():
    s = mx_kscale(DIN)
    gain = np.sqrt(np.mean(s * s))
    lim = 2.0 * np.sqrt(6.0 / (DIN + DOUT))
    m = np.random.standard_normal(DIN)
    g = (np.random.standard_normal((N, DIN)) + 0.5 * m) * s
    r = 0.3 + 0.68 * np.random.random_sample((N, 1))
    w0 = np.random.uniform(-lim, lim, (DOUT, DIN))
    wm = w0 @ m
    b = wm / np.linalg.norm(wm) + np.random.standard_normal(DOUT) / np.sqrt(DOUT)
    words, scales = pack_weight((w0 * gain / s).T, "e4m3")
    return {"x": bf(g / np.linalg.norm(g, axis=-1, keepdims=True) * r), "weight_words": words, "weight_scales": scales, "bias": bf(0.35 * b)}


def reference(x, weight_words, weight_scales, bias):
    c = C
    res = mobius_matvec(unpack_weight(weight_words, weight_scales, "e4m3").T, f64(x), c)
    res = project(res, c)
    hyp_bias = project(expmap0(f64(bias)[None, :], c), c)
    res = project(mobius_add(res, hyp_bias, c), c)
    return res

@@ -1,0 +1,243 @@
+from contextlib import ExitStack
+
+import concourse.mybir as mybir
+from concourse.masks import make_identity
+
+F32 = mybir.dt.float32
+BF16 = mybir.dt.bfloat16
+I32 = mybir.dt.int32
+U32 = mybir.dt.uint32
+U8 = mybir.dt.uint8
+FP8X4 = mybir.dt.float8_e4m3fn_x4
+ALU = mybir.AluOpType
+ACTF = mybir.ActivationFunctionType
+AX = mybir.AxisListType
+
+P = 128
+DIN = 4096
+DOUT = 4096
+G = DIN // 512
+NT = 512
+NB = DOUT // NT
+G_FULL = 6
+MAXN = 0.996
+MIN_NORM = 1e-15
+
+FLOPS = 2 * 128 * DIN * DOUT
+
+
+def tile_hyplinear_w_kernel(tc, x, weight_words, weight_scales, bias, out):
+    nc = tc.nc
+    with ExitStack() as ctx:
+        ctx.enter_context(tc.manual_schedule())
+        keep = ctx.enter_context(tc.tile_pool(name="keep", bufs=1))
+        work = ctx.enter_context(tc.tile_pool(name="work", bufs=3))
+        psum = ctx.enter_context(tc.psum_pool(name="psum", bufs=1))
+
+        x_sb = keep.tile([P, DIN], BF16, name="x_sb", align_bytes=64)
+        grouped = keep.tile([P, G, P, 4], BF16, name="grouped", align_bytes=64)
+        xq = keep.tile([P, G * P], U32, name="xq", align_bytes=64)
+        xs = keep.tile([P, G * P], U8, name="xs", align_bytes=64)
+        planes = [keep.tile([P, DOUT], U8, name="planes%d" % h, align_bytes=64) for h in range(2)]
+        w_full = [keep.tile([P, 4 * DOUT], U8, name="w%d" % g, align_bytes=64) for g in range(G_FULL)]
+        w_tail = keep.tile([P, G - G_FULL, 4 * DOUT], U8, name="w_tail", align_bytes=64)
+        brow = keep.tile([P, DOUT], BF16, name="brow")
+        b_bc = keep.tile([P, DOUT], BF16, name="b_bc")
+        junkbig = keep.tile([P, DOUT], BF16, name="junkbig")
+        o_sb = keep.tile([P, DOUT], F32, name="o_sb")
+        ones = keep.tile([P, P], BF16, name="ones")
+        ident = keep.tile([P, P], F32, name="ident")
+        e4 = keep.tile([P, 4], F32, name="e4")
+        em = keep.tile([P, 2], F32, name="em")
+
+        sxb = keep.tile([P, 2], F32, name="sxb")
+        n4 = keep.tile([P, 4], F32, name="n4")
+        pw4 = keep.tile([P, 4], F32, name="pw4")
+        ev = keep.tile([P, 16], F32, name="ev")
+        ll = keep.tile([P, 2], F32, name="ll")
+        tb = keep.tile([P, 1], F32, name="tb")
+        s1p = keep.tile([P, NB], F32, name="s1p")
+        s2p = keep.tile([P, NB], F32, name="s2p")
+        gp = keep.tile([P, NB], F32, name="gp")
+        m2 = keep.tile([P, 2], F32, name="m2")
+        pw = keep.tile([P, 2], F32, name="pw")
+        tt = keep.tile([P, 1], F32, name="tt")
+        lv = keep.tile([P, 16], F32, name="lv")
+        ds = keep.tile([P, 2], F32, name="ds")
+        rr = keep.tile([P, 2], F32, name="rr")
+        pq = keep.tile([P, 2], F32, name="pq")
+        ab = keep.tile([P, 2], F32, name="ab")
+
+        make_identity(nc, ident[:])
+        nc.sync.dma_start(out=x_sb[:], in_=x)
+        nc.vector.memset(brow[:].bitcast(I32), 0)
+        for h in range(2):
+            nc.vector.memset(planes[h][:].bitcast(I32), 0)
+        nc.vector.memset(ones[:], 1.0)
+        nc.vector.memset(e4[:, 0:1], 0.5)
+        nc.vector.memset(e4[:, 1:2], -0.5)
+        nc.vector.memset(e4[:, 2:3], 0.5)
+        nc.vector.memset(e4[:, 3:4], -0.5)
+        nc.vector.memset(em[:], -0.5)
+
+        nc.scalar.dma_start(out=brow[0:1, :], in_=bias.unsqueeze(0))
+        for h in range(2):
+            for q in range(4):
+                nc.sync.dma_start(
+                    out=planes[h][32 * q : 32 * q + 16, :].bitcast(I32),
+                    in_=weight_scales[4 * h : 4 * h + 4, 4 * q : 4 * q + 4, :].bitcast(I32),
+                )
+        for g in range(G_FULL):
+            nc.sync.dma_start(
+                out=w_full[g][:].bitcast(I32),
+                in_=weight_words[g].rearrange("p n t -> p (n t)").bitcast(I32),
+            )
+        tail_src = weight_words[G_FULL:G].rearrange("g p n t -> p g (n t)")
+        for r in range(3):
+            cols = slice(4 * 1024 * r, 4 * 1024 * (r + 1))
+            nc.sync.dma_start(out=w_tail[:, :, cols].bitcast(I32), in_=tail_src[:, :, cols].bitcast(I32))
+        nc.sync.dma_start(
+            out=w_tail[:, 0, 4 * 3072 :].bitcast(I32), in_=tail_src[:, 0, 4 * 3072 :].bitcast(I32)
+        )
+        for j in (6, 7):
+            cols = slice(4 * NT * j, 4 * NT * (j + 1))
+            nc.sync.dma_start(out=w_tail[:, 1, cols].bitcast(I32), in_=tail_src[:, 1, cols].bitcast(I32))
+
+        x32 = x_sb[:].bitcast(F32)
+        g32 = grouped[:].bitcast(F32)
+        xts = []
+        for k in range(4):
+            xt = psum.tile([P, 2, 2, P], F32, name="xt%d" % k, tag="bank%d" % k)
+            xts.append(xt)
+            for gi in range(2):
+                g = 2 * k + gi
+                for u in range(2):
+                    nc.tensor.transpose(xt[:, gi, u, :], x32[:, 256 * g + u : 256 * (g + 1) : 2], ident[:])
+        for k in range(4):
+            src = xts[k][:].rearrange("p g u m -> p g m u")
+            dst = g32[:, 2 * k : 2 * k + 2, :, :]
+            if k % 2 == 0:
+                nc.vector.tensor_copy(out=dst, in_=src)
+            else:
+                nc.scalar.copy(out=dst, in_=src)
+        for h in range(2):
+            nc.vector.quantize_mx(
+                out=xq[:, 512 * h : 512 * (h + 1)].bitcast(FP8X4),
+                scales=xs[:, 512 * h : 512 * (h + 1)],
+                in_=grouped[:, 4 * h : 4 * h + 4, :, :].rearrange("p g m t -> p (g m t)"),
+            )
+
+        for k in range(4):
+            bb = psum.tile([P, 2 * NT], BF16, name="bb%d" % k, tag="bank%d" % (4 + k))
+            for i in range(2):
+                c0 = 2 * NT * k + NT * i
+                nc.tensor.matmul(
+                    bb[:, NT * i : NT * (i + 1)], lhsT=ones[:], rhs=brow[:, c0 : c0 + NT], start=True, stop=True
+                )
+            dst = b_bc[:, 2 * NT * k : 2 * NT * (k + 1)]
+            if k % 2 == 0:
+                nc.scalar.copy(out=dst, in_=bb[:])
+            else:
+                nc.vector.tensor_copy(out=dst, in_=bb[:])
+
+        nc.scalar.activation(out=junkbig[:], in_=x_sb[:], func=ACTF.Square, accum_out=sxb[:, 0:1])
+        nc.scalar.activation(out=junkbig[:], in_=b_bc[:], func=ACTF.Square, accum_out=sxb[:, 1:2])
+        for i in range(2):
+            nc.vector.tensor_scalar(
+                out=n4[:, 2 * i : 2 * i + 2], in0=sxb[:, i : i + 1].to_broadcast([P, 2]),
+                scalar1=MIN_NORM, scalar2=None, op0=ALU.max,
+            )
+        nc.gpsimd.tensor_tensor(out=pw4[:], in0=n4[:], in1=e4[:], op=ALU.pow)
+        um, up, dl, cc, gam, y2, y2m1, g2, ng = (
+            ev[:, 0:1], ev[:, 1:3], ev[:, 3:4], ev[:, 4:5], ev[:, 5:6], ev[:, 6:7], ev[:, 7:8], ev[:, 8:9], ev[:, 9:10],
+        )
+        nc.vector.tensor_scalar(out=um, in0=pw4[:, 0:1], scalar1=1.0 - 1e-5, scalar2=None, op0=ALU.min)
+        nc.vector.tensor_scalar(out=up[:, 0:1], in0=um, scalar1=1.0, scalar2=None, op0=ALU.add)
+        nc.vector.tensor_scalar(out=up[:, 1:2], in0=um, scalar1=-1.0, scalar2=1.0, op0=ALU.mult, op1=ALU.add)
+        nc.scalar.activation(out=ll[:], in_=up, func=ACTF.Ln)
+        nc.scalar.activation(out=tb[:], in_=pw4[:, 2:3], func=ACTF.Tanh)
+        nc.vector.tensor_tensor(out=dl, in0=ll[:, 0:1], in1=ll[:, 1:2], op=ALU.subtract)
+        nc.vector.tensor_scalar(out=cc, in0=dl, scalar1=pw4[:, 1:2], scalar2=0.5, op0=ALU.mult, op1=ALU.mult)
+        nc.vector.tensor_scalar(out=gam, in0=tb[:], scalar1=MAXN, scalar2=pw4[:, 3:4], op0=ALU.min, op1=ALU.mult)
+        nc.vector.tensor_scalar(out=y2, in0=gam, scalar1=gam, scalar2=sxb[:, 1:2], op0=ALU.mult, op1=ALU.mult)
+        nc.vector.tensor_scalar(out=y2m1, in0=y2, scalar1=-1.0, scalar2=None, op0=ALU.add)
+        nc.vector.tensor_scalar(out=g2, in0=gam, scalar1=2.0, scalar2=None, op0=ALU.mult)
+        nc.vector.tensor_scalar(out=ng, in0=gam, scalar1=-1.0, scalar2=None, op0=ALU.mult)
+
+        acc = [psum.tile([P, NT], F32, name="acc%d" % j, tag="bank%d" % j) for j in range(NB)]
+
+        def mx_pass(g, j):
+            if g < G_FULL:
+                words = w_full[g][:, 4 * NT * j : 4 * NT * (j + 1)]
+            else:
+                words = w_tail[:, g - G_FULL, 4 * NT * j : 4 * NT * (j + 1)]
+            nc.tensor.matmul_mx(
+                out=acc[j][:],
+                lhsT=xq[:, P * g : P * (g + 1)].bitcast(FP8X4),
+                lhsT_scale=xs[:, P * g : P * (g + 1)],
+                rhs=words.bitcast(FP8X4),
+                rhs_scale=planes[g // 4][4 * (g % 4) : P, NT * j : NT * (j + 1)],
+                start=(g == 0),
+                stop=(g == G - 1),
+            )
+
+        def sums(j):
+            junk = work.tile([P, NT], F32, name="junk", tag="junk")
+            nc.scalar.activation(out=junk[:], in_=acc[j][:], func=ACTF.Square, accum_out=s1p[:, j : j + 1])
+            if j == 1:
+                nc.gpsimd.tensor_tensor(out=gp[:, 1:2], in0=s1p[:, 0:1], in1=s1p[:, 1:2], op=ALU.add)
+            elif 1 < j < NB - 1:
+                nc.gpsimd.tensor_tensor(out=gp[:, j : j + 1], in0=gp[:, j - 1 : j], in1=s1p[:, j : j + 1], op=ALU.add)
+            nc.vector.scalar_tensor_tensor(
+                out=junk[:], in0=acc[j][:], scalar=1.0, in1=b_bc[:, NT * j : NT * (j + 1)],
+                op0=ALU.mult, op1=ALU.mult, accum_out=s2p[:, j : j + 1],
+            )
+
+        for g in range(G_FULL):
+            for j in range(NB):
+                mx_pass(g, j)
+        for r in range(3):
+            for j in (2 * r, 2 * r + 1):
+                mx_pass(6, j)
+                mx_pass(7, j)
+            for j in (2 * r, 2 * r + 1):
+                sums(j)
+        mx_pass(6, 6)
+        mx_pass(6, 7)
+        mx_pass(7, 6)
+        mx_pass(7, 7)
+        sums(6)
+        pre2, sg, rho2, tp, a1, qq, ar, uu = (
+            lv[:, 0:1], lv[:, 1:2], lv[:, 2:3], lv[:, 3:4], lv[:, 4:5], lv[:, 5:6], lv[:, 6:7], lv[:, 7:8],
+        )
+        nc.vector.tensor_reduce(out=pre2, in_=s2p[:, 0 : NB - 1], axis=AX.X, op=ALU.add)
+        sums(7)
+
+        nc.gpsimd.tensor_scalar(
+            out=m2[:], in0=s1p[:, NB - 1 : NB].to_broadcast([P, 2]), scalar1=gp[:, NB - 2 : NB - 1],
+            scalar2=MIN_NORM, op0=ALU.add, op1=ALU.max,
+        )
+        nc.gpsimd.tensor_tensor(out=pw[:], in0=m2[:], in1=e4[:, 0:2], op=ALU.pow)
+        nc.scalar.activation(out=tt[:], in_=pw[:, 0:1], func=ACTF.Tanh, scale=cc)
+        nc.vector.tensor_scalar(out=sg, in0=s2p[:, NB - 1 : NB], scalar1=pre2, scalar2=g2, op0=ALU.add, op1=ALU.mult)
+        nc.vector.tensor_tensor(out=rho2, in0=sg, in1=pw[:, 1:2], op=ALU.mult)
+        nc.vector.tensor_scalar(out=tp, in0=tt[:], scalar1=MAXN, scalar2=None, op0=ALU.min)
+        nc.vector.tensor_scalar(out=a1, in0=tp, scalar1=rho2, scalar2=1.0, op0=ALU.mult, op1=ALU.add)
+        nc.vector.tensor_tensor(out=qq, in0=tp, in1=tp, op=ALU.mult)
+        nc.vector.tensor_scalar(out=ds[:, 0:1], in0=qq, scalar1=y2, scalar2=a1, op0=ALU.mult, op1=ALU.add)
+        nc.vector.tensor_scalar(out=ds[:, 1:2], in0=qq, scalar1=a1, scalar2=y2m1, op0=ALU.add, op1=ALU.add)
+        nc.gpsimd.tensor_tensor(out=rr[:], in0=ds[:], in1=em[:], op=ALU.pow)
+        nc.vector.tensor_tensor(out=ar, in0=tp, in1=pw[:, 1:2], op=ALU.mult)
+        nc.vector.tensor_scalar(out=pq[:, 0:1], in0=a1, scalar1=y2, scalar2=ar, op0=ALU.add, op1=ALU.mult)
+        nc.vector.tensor_scalar(out=pq[:, 1:2], in0=qq, scalar1=ng, scalar2=gam, op0=ALU.mult, op1=ALU.add)
+        nc.vector.tensor_scalar(out=uu, in0=rr[:, 1:2], scalar1=MAXN, scalar2=rr[:, 0:1], op0=ALU.mult, op1=ALU.min)
+        nc.vector.tensor_scalar(out=ab[:], in0=pq[:], scalar1=rr[:, 0:1], scalar2=uu, op0=ALU.mult, op1=ALU.mult)
+
+        for j in range(NB):
+            cols = slice(NT * j, NT * (j + 1))
+            bbt = work.tile([P, NT], F32, name="bbt", tag="bbt")
+            nc.scalar.activation(out=bbt[:], in_=b_bc[:, cols], func=ACTF.Copy, scale=ab[:, 1:2])
+            nc.vector.scalar_tensor_tensor(
+                out=o_sb[:, cols], in0=acc[j][:], scalar=ab[:, 0:1], in1=bbt[:], op0=ALU.mult, op1=ALU.add
+            )
+            nc.sync.dma_start(out=out[:, cols], in_=o_sb[:, cols])

@@ -70,9 +70,9 @@ def tile_hyplinear_w_kernel(tc, x, weight_words, weight_scales, bias, out):
 
         make_identity(nc, ident[:])
         nc.sync.dma_start(out=x_sb[:], in_=x)
+        nc.vector.memset(planes[0][:].bitcast(I32), 0)
         nc.vector.memset(brow[:].bitcast(I32), 0)
-        for h in range(2):
-            nc.vector.memset(planes[h][:].bitcast(I32), 0)
+        nc.vector.memset(planes[1][:].bitcast(I32), 0)
         nc.vector.memset(ones[:], 1.0)
         nc.vector.memset(e4[:, 0:1], 0.5)
         nc.vector.memset(e4[:, 1:2], -0.5)
@@ -80,28 +80,24 @@ def tile_hyplinear_w_kernel(tc, x, weight_words, weight_scales, bias, out):
         nc.vector.memset(e4[:, 3:4], -0.5)
         nc.vector.memset(em[:], -0.5)
 
-        nc.scalar.dma_start(out=brow[0:1, :], in_=bias.unsqueeze(0))
-        for h in range(2):
+        def load_planes(h):
             for q in range(4):
-                nc.sync.dma_start(
-                    out=planes[h][32 * q : 32 * q + 16, :].bitcast(I32),
-                    in_=weight_scales[4 * h : 4 * h + 4, 4 * q : 4 * q + 4, :].bitcast(I32),
+                nc.scalar.dma_start(
+                    out=planes[h][32 * q : 32 * q + 16, :].bitcast(F32),
+                    in_=weight_scales[4 * h : 4 * h + 4, 4 * q : 4 * q + 4, :].bitcast(F32),
                 )
-        for g in range(G_FULL):
+
+        def load_group(g):
             nc.sync.dma_start(
                 out=w_full[g][:].bitcast(I32),
                 in_=weight_words[g].rearrange("p n t -> p (n t)").bitcast(I32),
             )
-        tail_src = weight_words[G_FULL:G].rearrange("g p n t -> p g (n t)")
-        for r in range(3):
-            cols = slice(4 * 1024 * r, 4 * 1024 * (r + 1))
-            nc.sync.dma_start(out=w_tail[:, :, cols].bitcast(I32), in_=tail_src[:, :, cols].bitcast(I32))
-        nc.sync.dma_start(
-            out=w_tail[:, 0, 4 * 3072 :].bitcast(I32), in_=tail_src[:, 0, 4 * 3072 :].bitcast(I32)
-        )
-        for j in (6, 7):
-            cols = slice(4 * NT * j, 4 * NT * (j + 1))
-            nc.sync.dma_start(out=w_tail[:, 1, cols].bitcast(I32), in_=tail_src[:, 1, cols].bitcast(I32))
+
+        load_group(0)
+        load_planes(0)
+        nc.scalar.dma_start(out=brow[0:1, :], in_=bias.unsqueeze(0))
+        for g in range(1, 4):
+            load_group(g)
 
         x32 = x_sb[:].bitcast(F32)
         g32 = grouped[:].bitcast(F32)
@@ -141,6 +137,19 @@ def tile_hyplinear_w_kernel(tc, x, weight_words, weight_scales, bias, out):
                 nc.vector.tensor_copy(out=dst, in_=bb[:])
 
         nc.scalar.activation(out=junkbig[:], in_=x_sb[:], func=ACTF.Square, accum_out=sxb[:, 0:1])
+        load_planes(1)
+        for g in range(4, G_FULL):
+            load_group(g)
+        tail_src = weight_words[G_FULL:G].rearrange("g p n t -> p g (n t)")
+        for r in range(3):
+            cols = slice(4 * 1024 * r, 4 * 1024 * (r + 1))
+            nc.sync.dma_start(out=w_tail[:, :, cols].bitcast(I32), in_=tail_src[:, :, cols].bitcast(I32))
+        nc.sync.dma_start(
+            out=w_tail[:, 0, 4 * 3072 :].bitcast(I32), in_=tail_src[:, 0, 4 * 3072 :].bitcast(I32)
+        )
+        for j in (6, 7):
+            cols = slice(4 * NT * j, 4 * NT * (j + 1))
+            nc.sync.dma_start(out=w_tail[:, 1, cols].bitcast(I32), in_=tail_src[:, 1, cols].bitcast(I32))
         nc.scalar.activation(out=junkbig[:], in_=b_bc[:], func=ACTF.Square, accum_out=sxb[:, 1:2])
         for i in range(2):
             nc.vector.tensor_scalar(

@@ -70,9 +70,9 @@ def tile_hyplinear_w_kernel(tc, x, weight_words, weight_scales, bias, out):
 
         make_identity(nc, ident[:])
         nc.sync.dma_start(out=x_sb[:], in_=x)
-        nc.vector.memset(planes[0][:].bitcast(I32), 0)
+        for h in range(2):
+            nc.vector.memset(planes[h][:].bitcast(I32), 0)
         nc.vector.memset(brow[:].bitcast(I32), 0)
-        nc.vector.memset(planes[1][:].bitcast(I32), 0)
         nc.vector.memset(ones[:], 1.0)
         nc.vector.memset(e4[:, 0:1], 0.5)
         nc.vector.memset(e4[:, 1:2], -0.5)
@@ -80,24 +80,30 @@ def tile_hyplinear_w_kernel(tc, x, weight_words, weight_scales, bias, out):
         nc.vector.memset(e4[:, 3:4], -0.5)
         nc.vector.memset(em[:], -0.5)
 
-        def load_planes(h):
+        nc.scalar.dma_start(out=brow[0:1, :], in_=bias.unsqueeze(0))
+        for h in range(2):
             for q in range(4):
-                nc.scalar.dma_start(
+                nc.gpsimd.dma_start(
                     out=planes[h][32 * q : 32 * q + 16, :].bitcast(F32),
                     in_=weight_scales[4 * h : 4 * h + 4, 4 * q : 4 * q + 4, :].bitcast(F32),
                 )
-
-        def load_group(g):
-            nc.sync.dma_start(
-                out=w_full[g][:].bitcast(I32),
-                in_=weight_words[g].rearrange("p n t -> p (n t)").bitcast(I32),
-            )
-
-        load_group(0)
-        load_planes(0)
-        nc.scalar.dma_start(out=brow[0:1, :], in_=bias.unsqueeze(0))
-        for g in range(1, 4):
-            load_group(g)
+        for g in range(G_FULL):
+            src_g = weight_words[g].rearrange("p n t -> p (n t)")
+            pieces = 2 if g < 2 else 1
+            width = 4 * DOUT // pieces
+            for i in range(pieces):
+                cols = slice(width * i, width * (i + 1))
+                nc.sync.dma_start(out=w_full[g][:, cols].bitcast(I32), in_=src_g[:, cols].bitcast(I32))
+        tail_src = weight_words[G_FULL:G].rearrange("g p n t -> p g (n t)")
+        for r in range(3):
+            cols = slice(4 * 1024 * r, 4 * 1024 * (r + 1))
+            nc.sync.dma_start(out=w_tail[:, :, cols].bitcast(I32), in_=tail_src[:, :, cols].bitcast(I32))
+        nc.sync.dma_start(
+            out=w_tail[:, 0, 4 * 3072 :].bitcast(I32), in_=tail_src[:, 0, 4 * 3072 :].bitcast(I32)
+        )
+        for j in (6, 7):
+            cols = slice(4 * NT * j, 4 * NT * (j + 1))
+            nc.sync.dma_start(out=w_tail[:, 1, cols].bitcast(I32), in_=tail_src[:, 1, cols].bitcast(I32))
 
         x32 = x_sb[:].bitcast(F32)
         g32 = grouped[:].bitcast(F32)
@@ -137,19 +143,6 @@ def tile_hyplinear_w_kernel(tc, x, weight_words, weight_scales, bias, out):
                 nc.vector.tensor_copy(out=dst, in_=bb[:])
 
         nc.scalar.activation(out=junkbig[:], in_=x_sb[:], func=ACTF.Square, accum_out=sxb[:, 0:1])
-        load_planes(1)
-        for g in range(4, G_FULL):
-            load_group(g)
-        tail_src = weight_words[G_FULL:G].rearrange("g p n t -> p g (n t)")
-        for r in range(3):
-            cols = slice(4 * 1024 * r, 4 * 1024 * (r + 1))
-            nc.sync.dma_start(out=w_tail[:, :, cols].bitcast(I32), in_=tail_src[:, :, cols].bitcast(I32))
-        nc.sync.dma_start(
-            out=w_tail[:, 0, 4 * 3072 :].bitcast(I32), in_=tail_src[:, 0, 4 * 3072 :].bitcast(I32)
-        )
-        for j in (6, 7):
-            cols = slice(4 * NT * j, 4 * NT * (j + 1))
-            nc.sync.dma_start(out=w_tail[:, 1, cols].bitcast(I32), in_=tail_src[:, 1, cols].bitcast(I32))
         nc.scalar.activation(out=junkbig[:], in_=b_bc[:], func=ACTF.Square, accum_out=sxb[:, 1:2])
         for i in range(2):
             nc.vector.tensor_scalar(

@@ -59,20 +59,20 @@ def tile_hyplinear_w_kernel(tc, x, weight_words, weight_scales, bias, out):
         s1p = keep.tile([P, NB], F32, name="s1p")
         s2p = keep.tile([P, NB], F32, name="s2p")
         gp = keep.tile([P, NB], F32, name="gp")
-        m2 = keep.tile([P, 2], F32, name="m2")
-        pw = keep.tile([P, 2], F32, name="pw")
+        m1 = keep.tile([P, 1], F32, name="m1")
+        sq = keep.tile([P, 1], F32, name="sq")
         tt = keep.tile([P, 1], F32, name="tt")
         lv = keep.tile([P, 16], F32, name="lv")
-        ds = keep.tile([P, 2], F32, name="ds")
-        rr = keep.tile([P, 2], F32, name="rr")
+        rsd = keep.tile([P, 1], F32, name="rsd")
+        bbt = keep.tile([P, DOUT], F32, name="bbt")
         pq = keep.tile([P, 2], F32, name="pq")
         ab = keep.tile([P, 2], F32, name="ab")
 
         make_identity(nc, ident[:])
         nc.sync.dma_start(out=x_sb[:], in_=x)
+        nc.vector.memset(brow[:].bitcast(I32), 0)
         for h in range(2):
             nc.vector.memset(planes[h][:].bitcast(I32), 0)
-        nc.vector.memset(brow[:].bitcast(I32), 0)
         nc.vector.memset(ones[:], 1.0)
         nc.vector.memset(e4[:, 0:1], 0.5)
         nc.vector.memset(e4[:, 1:2], -0.5)
@@ -83,17 +83,15 @@ def tile_hyplinear_w_kernel(tc, x, weight_words, weight_scales, bias, out):
         nc.scalar.dma_start(out=brow[0:1, :], in_=bias.unsqueeze(0))
         for h in range(2):
             for q in range(4):
-                nc.gpsimd.dma_start(
-                    out=planes[h][32 * q : 32 * q + 16, :].bitcast(F32),
-                    in_=weight_scales[4 * h : 4 * h + 4, 4 * q : 4 * q + 4, :].bitcast(F32),
+                nc.sync.dma_start(
+                    out=planes[h][32 * q : 32 * q + 16, :].bitcast(I32),
+                    in_=weight_scales[4 * h : 4 * h + 4, 4 * q : 4 * q + 4, :].bitcast(I32),
                 )
         for g in range(G_FULL):
-            src_g = weight_words[g].rearrange("p n t -> p (n t)")
-            pieces = 2 if g < 2 else 1
-            width = 4 * DOUT // pieces
-            for i in range(pieces):
-                cols = slice(width * i, width * (i + 1))
-                nc.sync.dma_start(out=w_full[g][:, cols].bitcast(I32), in_=src_g[:, cols].bitcast(I32))
+            nc.sync.dma_start(
+                out=w_full[g][:].bitcast(I32),
+                in_=weight_words[g].rearrange("p n t -> p (n t)").bitcast(I32),
+            )
         tail_src = weight_words[G_FULL:G].rearrange("g p n t -> p g (n t)")
         for r in range(3):
             cols = slice(4 * 1024 * r, 4 * 1024 * (r + 1))
@@ -209,37 +207,56 @@ def tile_hyplinear_w_kernel(tc, x, weight_words, weight_scales, bias, out):
         mx_pass(7, 6)
         mx_pass(7, 7)
         sums(6)
-        pre2, sg, rho2, tp, a1, qq, ar, uu = (
+        pre2, sg, rho2, tp, a1, qq, ar, hh, rn, den, ss, sd, rden = (
             lv[:, 0:1], lv[:, 1:2], lv[:, 2:3], lv[:, 3:4], lv[:, 4:5], lv[:, 5:6], lv[:, 6:7], lv[:, 7:8],
+            lv[:, 8:9], lv[:, 9:10], lv[:, 10:11], lv[:, 11:12], lv[:, 12:13],
         )
         nc.vector.tensor_reduce(out=pre2, in_=s2p[:, 0 : NB - 1], axis=AX.X, op=ALU.add)
         sums(7)
 
         nc.gpsimd.tensor_scalar(
-            out=m2[:], in0=s1p[:, NB - 1 : NB].to_broadcast([P, 2]), scalar1=gp[:, NB - 2 : NB - 1],
+            out=m1[:], in0=s1p[:, NB - 1 : NB], scalar1=gp[:, NB - 2 : NB - 1],
             scalar2=MIN_NORM, op0=ALU.add, op1=ALU.max,
         )
-        nc.gpsimd.tensor_tensor(out=pw[:], in0=m2[:], in1=e4[:, 0:2], op=ALU.pow)
-        nc.scalar.activation(out=tt[:], in_=pw[:, 0:1], func=ACTF.Tanh, scale=cc)
+        nc.gpsimd.tensor_tensor(out=sq[:], in0=m1[:], in1=e4[:, 0:1], op=ALU.pow)
+        nc.scalar.activation(out=tt[:], in_=sq[:], func=ACTF.Tanh, scale=cc)
         nc.vector.tensor_scalar(out=sg, in0=s2p[:, NB - 1 : NB], scalar1=pre2, scalar2=g2, op0=ALU.add, op1=ALU.mult)
-        nc.vector.tensor_tensor(out=rho2, in0=sg, in1=pw[:, 1:2], op=ALU.mult)
+        nc.vector.reciprocal(out=rn, in_=sq[:])
+        nc.vector.tensor_tensor(out=rho2, in0=sg, in1=rn, op=ALU.mult)
         nc.vector.tensor_scalar(out=tp, in0=tt[:], scalar1=MAXN, scalar2=None, op0=ALU.min)
         nc.vector.tensor_scalar(out=a1, in0=tp, scalar1=rho2, scalar2=1.0, op0=ALU.mult, op1=ALU.add)
         nc.vector.tensor_tensor(out=qq, in0=tp, in1=tp, op=ALU.mult)
-        nc.vector.tensor_scalar(out=ds[:, 0:1], in0=qq, scalar1=y2, scalar2=a1, op0=ALU.mult, op1=ALU.add)
-        nc.vector.tensor_scalar(out=ds[:, 1:2], in0=qq, scalar1=a1, scalar2=y2m1, op0=ALU.add, op1=ALU.add)
-        nc.gpsimd.tensor_tensor(out=rr[:], in0=ds[:], in1=em[:], op=ALU.pow)
-        nc.vector.tensor_tensor(out=ar, in0=tp, in1=pw[:, 1:2], op=ALU.mult)
+        nc.vector.tensor_scalar(out=den, in0=qq, scalar1=y2, scalar2=a1, op0=ALU.mult, op1=ALU.add)
+        nc.vector.tensor_scalar(out=ss, in0=qq, scalar1=a1, scalar2=y2m1, op0=ALU.add, op1=ALU.add)
+        nc.vector.tensor_tensor(out=sd, in0=ss, in1=den, op=ALU.mult)
+        nc.gpsimd.tensor_tensor(out=rsd[:], in0=sd, in1=em[:, 0:1], op=ALU.pow)
+        nc.vector.reciprocal(out=rden, in_=den)
+        nc.vector.tensor_tensor(out=ar, in0=tp, in1=rn, op=ALU.mult)
         nc.vector.tensor_scalar(out=pq[:, 0:1], in0=a1, scalar1=y2, scalar2=ar, op0=ALU.add, op1=ALU.mult)
         nc.vector.tensor_scalar(out=pq[:, 1:2], in0=qq, scalar1=ng, scalar2=gam, op0=ALU.mult, op1=ALU.add)
-        nc.vector.tensor_scalar(out=uu, in0=rr[:, 1:2], scalar1=MAXN, scalar2=rr[:, 0:1], op0=ALU.mult, op1=ALU.min)
-        nc.vector.tensor_scalar(out=ab[:], in0=pq[:], scalar1=rr[:, 0:1], scalar2=uu, op0=ALU.mult, op1=ALU.mult)
+        nc.vector.tensor_scalar(out=hh, in0=rsd[:], scalar1=MAXN, scalar2=rden, op0=ALU.mult, op1=ALU.min)
+        nc.vector.tensor_scalar(out=ab[:], in0=pq[:], scalar1=hh, scalar2=None, op0=ALU.mult)
 
-        for j in range(NB):
-            cols = slice(NT * j, NT * (j + 1))
-            bbt = work.tile([P, NT], F32, name="bbt", tag="bbt")
-            nc.scalar.activation(out=bbt[:], in_=b_bc[:, cols], func=ACTF.Copy, scale=ab[:, 1:2])
+        chunks = [(0, 128, "v"), (128, 128, "s"), (256, 256, "s")]
+        for j in range(1, NB - 1):
+            chunks.append((NT * j, NT, "g" if j % 2 == 1 else "s"))
+        chunks.append((NT * (NB - 1), 256, "g"))
+        chunks.append((NT * (NB - 1) + 256, 256, "g"))
+        for c0, width, who in chunks:
+            cols = slice(c0, c0 + width)
+            if who == "v":
+                nc.vector.tensor_scalar(out=bbt[:, cols], in0=b_bc[:, cols], scalar1=ab[:, 1:2], scalar2=None, op0=ALU.mult)
+            elif who == "s":
+                nc.scalar.activation(out=bbt[:, cols], in_=b_bc[:, cols], func=ACTF.Copy, scale=ab[:, 1:2])
+            else:
+                nc.gpsimd.tensor_scalar(
+                    out=bbt[:, cols], in0=b_bc[:, cols], scalar1=ab[:, 1:2], scalar2=0.0, op0=ALU.mult, op1=ALU.add
+                )
+        for c0, width, who in chunks:
+            cols = slice(c0, c0 + width)
+            j = c0 // NT
             nc.vector.scalar_tensor_tensor(
-                out=o_sb[:, cols], in0=acc[j][:], scalar=ab[:, 0:1], in1=bbt[:], op0=ALU.mult, op1=ALU.add
+                out=o_sb[:, cols], in0=acc[j][:, c0 - NT * j : c0 - NT * j + width], scalar=ab[:, 0:1],
+                in1=bbt[:, cols], op0=ALU.mult, op1=ALU.add,
             )
             nc.sync.dma_start(out=out[:, cols], in_=o_sb[:, cols])

@@ -22,6 +22,9 @@ NB = DOUT // NT
 G_FULL = 6
 MAXN = 0.996
 MIN_NORM = 1e-15
+CINV = 1.0 / (MAXN * MAXN)
+Z0 = 3.1063030478757594
+BIG = 2.0 ** 100
 
 FLOPS = 2 * 128 * DIN * DOUT
 
@@ -58,15 +61,22 @@ def tile_hyplinear_w_kernel(tc, x, weight_words, weight_scales, bias, out):
         tb = keep.tile([P, 1], F32, name="tb")
         s1p = keep.tile([P, NB], F32, name="s1p")
         s2p = keep.tile([P, NB], F32, name="s2p")
-        gp = keep.tile([P, NB], F32, name="gp")
-        m1 = keep.tile([P, 1], F32, name="m1")
-        sq = keep.tile([P, 1], F32, name="sq")
-        tt = keep.tile([P, 1], F32, name="tt")
-        lv = keep.tile([P, 16], F32, name="lv")
-        rsd = keep.tile([P, 1], F32, name="rsd")
-        bbt = keep.tile([P, DOUT], F32, name="bbt")
-        pq = keep.tile([P, 2], F32, name="pq")
-        ab = keep.tile([P, 2], F32, name="ab")
+        onec = keep.tile([P, 1], F32, name="onec")
+        ex2 = keep.tile([P, 2], F32, name="ex2")
+        const4 = keep.tile([P, 4], F32, name="const4")
+        k2 = keep.tile([P, 2], F32, name="k2")
+        g2p = keep.tile([P, 2], F32, name="g2p")
+        pc = keep.tile([P, 3], F32, name="pc")
+        bigz = keep.tile([P, 2], F32, name="bigz")
+        pab = keep.tile([P, 8], F32, name="pab")
+        m2 = keep.tile([P, 2], F32, name="m2")
+        pw2 = keep.tile([P, 2], F32, name="pw2")
+        coef4 = keep.tile([P, 4], F32, name="coef4")
+        w4 = keep.tile([P, 4], F32, name="lvl1")
+        ds = keep.tile([P, 2], F32, name="ds")
+        lv = keep.tile([P, 8], F32, name="lv")
+        hh = keep.tile([P, 1], F32, name="hh")
+        t_sb = keep.tile([P, DOUT], F32, name="t_sb")
 
         make_identity(nc, ident[:])
         nc.sync.dma_start(out=x_sb[:], in_=x)
@@ -79,6 +89,12 @@ def tile_hyplinear_w_kernel(tc, x, weight_words, weight_scales, bias, out):
         nc.vector.memset(e4[:, 2:3], 0.5)
         nc.vector.memset(e4[:, 3:4], -0.5)
         nc.vector.memset(em[:], -0.5)
+        nc.vector.memset(onec[:], 1.0)
+        nc.vector.memset(ex2[:, 0:1], -0.5)
+        nc.vector.memset(ex2[:, 1:2], 0.5)
+        nc.vector.memset(const4[:, 2:3], 0.0)
+        nc.vector.memset(const4[:, 3:4], -1.0)
+        nc.vector.memset(bigz[:, 0:1], BIG)
 
         nc.scalar.dma_start(out=brow[0:1, :], in_=bias.unsqueeze(0))
         for h in range(2):
@@ -148,9 +164,8 @@ def tile_hyplinear_w_kernel(tc, x, weight_words, weight_scales, bias, out):
                 scalar1=MIN_NORM, scalar2=None, op0=ALU.max,
             )
         nc.gpsimd.tensor_tensor(out=pw4[:], in0=n4[:], in1=e4[:], op=ALU.pow)
-        um, up, dl, cc, gam, y2, y2m1, g2, ng = (
-            ev[:, 0:1], ev[:, 1:3], ev[:, 3:4], ev[:, 4:5], ev[:, 5:6], ev[:, 6:7], ev[:, 7:8], ev[:, 8:9], ev[:, 9:10],
-        )
+        um, up, dl, cc, gam, rcc = ev[:, 0:1], ev[:, 1:3], ev[:, 3:4], ev[:, 4:5], ev[:, 5:6], ev[:, 6:7]
+        y2 = k2[:, 0:1]
         nc.vector.tensor_scalar(out=um, in0=pw4[:, 0:1], scalar1=1.0 - 1e-5, scalar2=None, op0=ALU.min)
         nc.vector.tensor_scalar(out=up[:, 0:1], in0=um, scalar1=1.0, scalar2=None, op0=ALU.add)
         nc.vector.tensor_scalar(out=up[:, 1:2], in0=um, scalar1=-1.0, scalar2=1.0, op0=ALU.mult, op1=ALU.add)
@@ -160,9 +175,14 @@ def tile_hyplinear_w_kernel(tc, x, weight_words, weight_scales, bias, out):
         nc.vector.tensor_scalar(out=cc, in0=dl, scalar1=pw4[:, 1:2], scalar2=0.5, op0=ALU.mult, op1=ALU.mult)
         nc.vector.tensor_scalar(out=gam, in0=tb[:], scalar1=MAXN, scalar2=pw4[:, 3:4], op0=ALU.min, op1=ALU.mult)
         nc.vector.tensor_scalar(out=y2, in0=gam, scalar1=gam, scalar2=sxb[:, 1:2], op0=ALU.mult, op1=ALU.mult)
-        nc.vector.tensor_scalar(out=y2m1, in0=y2, scalar1=-1.0, scalar2=None, op0=ALU.add)
-        nc.vector.tensor_scalar(out=g2, in0=gam, scalar1=2.0, scalar2=None, op0=ALU.mult)
-        nc.vector.tensor_scalar(out=ng, in0=gam, scalar1=-1.0, scalar2=None, op0=ALU.mult)
+        nc.vector.tensor_scalar(out=k2[:, 1:2], in0=onec[:], scalar1=CINV, scalar2=None, op0=ALU.mult)
+        nc.vector.tensor_scalar(out=const4[:, 0:1], in0=y2, scalar1=1.0, scalar2=None, op0=ALU.add)
+        nc.vector.tensor_scalar(out=const4[:, 1:2], in0=y2, scalar1=1.0, scalar2=CINV, op0=ALU.add, op1=ALU.mult)
+        nc.vector.tensor_scalar(out=g2p[:, 0:1], in0=gam, scalar1=2.0, scalar2=None, op0=ALU.mult)
+        nc.vector.tensor_scalar(out=g2p[:, 1:2], in0=gam, scalar1=2.0 * CINV, scalar2=None, op0=ALU.mult)
+        nc.vector.reciprocal(out=pc[:, 2:3], in_=gam)
+        nc.vector.reciprocal(out=rcc, in_=cc)
+        nc.vector.tensor_scalar(out=bigz[:, 1:2], in0=rcc, scalar1=rcc, scalar2=Z0 * Z0, op0=ALU.mult, op1=ALU.mult)
 
         acc = [psum.tile([P, NT], F32, name="acc%d" % j, tag="bank%d" % j) for j in range(NB)]
 
@@ -181,18 +201,18 @@ def tile_hyplinear_w_kernel(tc, x, weight_words, weight_scales, bias, out):
                 stop=(g == G - 1),
             )
 
-        def sums(j):
+        def sum_sq(j):
             junk = work.tile([P, NT], F32, name="junk", tag="junk")
             nc.scalar.activation(out=junk[:], in_=acc[j][:], func=ACTF.Square, accum_out=s1p[:, j : j + 1])
-            if j == 1:
-                nc.gpsimd.tensor_tensor(out=gp[:, 1:2], in0=s1p[:, 0:1], in1=s1p[:, 1:2], op=ALU.add)
-            elif 1 < j < NB - 1:
-                nc.gpsimd.tensor_tensor(out=gp[:, j : j + 1], in0=gp[:, j - 1 : j], in1=s1p[:, j : j + 1], op=ALU.add)
+
+        def sum_b(j):
+            junk = work.tile([P, NT], F32, name="junkv", tag="junkv")
             nc.vector.scalar_tensor_tensor(
                 out=junk[:], in0=acc[j][:], scalar=1.0, in1=b_bc[:, NT * j : NT * (j + 1)],
                 op0=ALU.mult, op1=ALU.mult, accum_out=s2p[:, j : j + 1],
             )
 
+        p05, pa, pb, pre2 = pab[:, 0:1], pab[:, 1:3], pab[:, 3:5], pab[:, 5:6]
         for g in range(G_FULL):
             for j in range(NB):
                 mx_pass(g, j)
@@ -201,62 +221,73 @@ def tile_hyplinear_w_kernel(tc, x, weight_words, weight_scales, bias, out):
                 mx_pass(6, j)
                 mx_pass(7, j)
             for j in (2 * r, 2 * r + 1):
-                sums(j)
+                sum_sq(j)
+                sum_b(j)
+        nc.vector.tensor_reduce(out=p05, in_=s1p[:, 0:6], axis=AX.X, op=ALU.add)
+        nc.vector.tensor_scalar(out=pa, in0=p05.to_broadcast([P, 2]), scalar1=MIN_NORM, scalar2=None, op0=ALU.max)
         mx_pass(6, 6)
         mx_pass(6, 7)
         mx_pass(7, 6)
         mx_pass(7, 7)
-        sums(6)
-        pre2, sg, rho2, tp, a1, qq, ar, hh, rn, den, ss, sd, rden = (
-            lv[:, 0:1], lv[:, 1:2], lv[:, 2:3], lv[:, 3:4], lv[:, 4:5], lv[:, 5:6], lv[:, 6:7], lv[:, 7:8],
-            lv[:, 8:9], lv[:, 9:10], lv[:, 10:11], lv[:, 11:12], lv[:, 12:13],
-        )
+        sum_sq(6)
+        sum_b(6)
         nc.vector.tensor_reduce(out=pre2, in_=s2p[:, 0 : NB - 1], axis=AX.X, op=ALU.add)
-        sums(7)
+        nc.vector.tensor_scalar(out=pb, in0=pa, scalar1=s1p[:, 6:7], scalar2=None, op0=ALU.add)
+        sum_sq(7)
 
-        nc.gpsimd.tensor_scalar(
-            out=m1[:], in0=s1p[:, NB - 1 : NB], scalar1=gp[:, NB - 2 : NB - 1],
-            scalar2=MIN_NORM, op0=ALU.add, op1=ALU.max,
+        rnq, mmx, pqn, qg, hq = lv[:, 0:1], lv[:, 1:2], lv[:, 2:3], lv[:, 3:4], lv[:, 4:5]
+        a1y, urg, nq = w4[:, 0:1], w4[:, 2:3], w4[:, 3:4]
+        nc.vector.scalar_tensor_tensor(
+            out=m2[:], in0=pb, scalar=s1p[:, NB - 1 : NB], in1=bigz[:], op0=ALU.add, op1=ALU.min
         )
-        nc.gpsimd.tensor_tensor(out=sq[:], in0=m1[:], in1=e4[:, 0:1], op=ALU.pow)
-        nc.scalar.activation(out=tt[:], in_=sq[:], func=ACTF.Tanh, scale=cc)
-        nc.vector.tensor_scalar(out=sg, in0=s2p[:, NB - 1 : NB], scalar1=pre2, scalar2=g2, op0=ALU.add, op1=ALU.mult)
-        nc.vector.reciprocal(out=rn, in_=sq[:])
-        nc.vector.tensor_tensor(out=rho2, in0=sg, in1=rn, op=ALU.mult)
-        nc.vector.tensor_scalar(out=tp, in0=tt[:], scalar1=MAXN, scalar2=None, op0=ALU.min)
-        nc.vector.tensor_scalar(out=a1, in0=tp, scalar1=rho2, scalar2=1.0, op0=ALU.mult, op1=ALU.add)
-        nc.vector.tensor_tensor(out=qq, in0=tp, in1=tp, op=ALU.mult)
-        nc.vector.tensor_scalar(out=den, in0=qq, scalar1=y2, scalar2=a1, op0=ALU.mult, op1=ALU.add)
-        nc.vector.tensor_scalar(out=ss, in0=qq, scalar1=a1, scalar2=y2m1, op0=ALU.add, op1=ALU.add)
-        nc.vector.tensor_tensor(out=sd, in0=ss, in1=den, op=ALU.mult)
-        nc.gpsimd.tensor_tensor(out=rsd[:], in0=sd, in1=em[:, 0:1], op=ALU.pow)
-        nc.vector.reciprocal(out=rden, in_=den)
-        nc.vector.tensor_tensor(out=ar, in0=tp, in1=rn, op=ALU.mult)
-        nc.vector.tensor_scalar(out=pq[:, 0:1], in0=a1, scalar1=y2, scalar2=ar, op0=ALU.add, op1=ALU.mult)
-        nc.vector.tensor_scalar(out=pq[:, 1:2], in0=qq, scalar1=ng, scalar2=gam, op0=ALU.mult, op1=ALU.add)
-        nc.vector.tensor_scalar(out=hh, in0=rsd[:], scalar1=MAXN, scalar2=rden, op0=ALU.mult, op1=ALU.min)
-        nc.vector.tensor_scalar(out=ab[:], in0=pq[:], scalar1=hh, scalar2=None, op0=ALU.mult)
+        sum_b(7)
+        nc.gpsimd.tensor_tensor(out=pw2[:], in0=m2[:], in1=ex2[:], op=ALU.pow)
+        nc.vector.scalar_tensor_tensor(
+            out=pc[:, 0:2], in0=s2p[:, NB - 1 : NB].to_broadcast([P, 2]), scalar=pre2, in1=g2p[:],
+            op0=ALU.add, op1=ALU.mult,
+        )
+        nc.scalar.activation(out=coef4[:, 3:4], in_=pw2[:, 1:2], func=ACTF.Tanh, scale=cc)
+        nc.vector.tensor_scalar(out=coef4[:, 0:3], in0=pc[:], scalar1=pw2[:, 0:1], scalar2=None, op0=ALU.mult)
+        nc.vector.scalar_tensor_tensor(
+            out=w4[:], in0=coef4[:], scalar=coef4[:, 3:4], in1=const4[:], op0=ALU.mult, op1=ALU.add
+        )
+        nc.vector.scalar_tensor_tensor(out=ds[:], in0=k2[:], scalar=nq, in1=w4[:, 0:2], op0=ALU.mult, op1=ALU.add)
+        nc.vector.reciprocal(out=rnq, in_=nq)
+        nc.vector.scalar_tensor_tensor(
+            out=mmx, in0=ds[:, 1:2], scalar=ds[:, 0:1], in1=ds[:, 0:1], op0=ALU.max, op1=ALU.mult
+        )
+        nc.gpsimd.tensor_tensor(out=hh[:], in0=mmx, in1=em[:, 0:1], op=ALU.pow)
+        nc.vector.scalar_tensor_tensor(out=pqn, in0=a1y, scalar=urg, in1=rnq, op0=ALU.mult, op1=ALU.mult)
+        nc.vector.tensor_tensor(out=qg, in0=nq, in1=gam, op=ALU.mult)
 
-        chunks = [(0, 128, "v"), (128, 128, "s"), (256, 256, "s")]
+        chunks = [(0, 128, "g"), (128, 128, "s"), (256, 256, "s")]
         for j in range(1, NB - 1):
-            chunks.append((NT * j, NT, "g" if j % 2 == 1 else "s"))
-        chunks.append((NT * (NB - 1), 256, "g"))
-        chunks.append((NT * (NB - 1) + 256, 256, "g"))
-        for c0, width, who in chunks:
-            cols = slice(c0, c0 + width)
-            if who == "v":
-                nc.vector.tensor_scalar(out=bbt[:, cols], in0=b_bc[:, cols], scalar1=ab[:, 1:2], scalar2=None, op0=ALU.mult)
-            elif who == "s":
-                nc.scalar.activation(out=bbt[:, cols], in_=b_bc[:, cols], func=ACTF.Copy, scale=ab[:, 1:2])
-            else:
-                nc.gpsimd.tensor_scalar(
-                    out=bbt[:, cols], in0=b_bc[:, cols], scalar1=ab[:, 1:2], scalar2=0.0, op0=ALU.mult, op1=ALU.add
-                )
-        for c0, width, who in chunks:
-            cols = slice(c0, c0 + width)
+            chunks.append((NT * j, NT, "g" if j % 2 == 0 else "s"))
+        chunks.append((NT * (NB - 1), 256, "s"))
+        chunks.append((NT * (NB - 1) + 256, 256, "s"))
+
+        def combine(c0, width):
             j = c0 // NT
             nc.vector.scalar_tensor_tensor(
-                out=o_sb[:, cols], in0=acc[j][:, c0 - NT * j : c0 - NT * j + width], scalar=ab[:, 0:1],
-                in1=bbt[:, cols], op0=ALU.mult, op1=ALU.add,
+                out=t_sb[:, c0 : c0 + width], in0=acc[j][:, c0 - NT * j : c0 - NT * j + width], scalar=pqn,
+                in1=b_bc[:, c0 : c0 + width], op0=ALU.mult, op1=ALU.subtract,
             )
+
+        def finish(c0, width, who):
+            cols = slice(c0, c0 + width)
+            if who == "s":
+                nc.scalar.activation(out=o_sb[:, cols], in_=t_sb[:, cols], func=ACTF.Copy, scale=hq)
+            else:
+                nc.gpsimd.tensor_scalar(
+                    out=o_sb[:, cols], in0=t_sb[:, cols], scalar1=qg, scalar2=hh[:], op0=ALU.mult, op1=ALU.mult
+                )
             nc.sync.dma_start(out=out[:, cols], in_=o_sb[:, cols])
+
+        for c0, width, who in chunks[:3]:
+            combine(c0, width)
+        nc.vector.tensor_tensor(out=hq, in0=hh[:], in1=qg, op=ALU.mult)
+        for c0, width, who in chunks[:3]:
+            finish(c0, width, who)
+        for c0, width, who in chunks[3:]:
+            combine(c0, width)
+            finish(c0, width, who)

@@ -80,9 +80,9 @@ def tile_hyplinear_w_kernel(tc, x, weight_words, weight_scales, bias, out):
 
         make_identity(nc, ident[:])
         nc.sync.dma_start(out=x_sb[:], in_=x)
-        nc.vector.memset(brow[:].bitcast(I32), 0)
         for h in range(2):
             nc.vector.memset(planes[h][:].bitcast(I32), 0)
+        nc.vector.memset(brow[:].bitcast(I32), 0)
         nc.vector.memset(ones[:], 1.0)
         nc.vector.memset(e4[:, 0:1], 0.5)
         nc.vector.memset(e4[:, 1:2], -0.5)
@@ -97,8 +97,8 @@ def tile_hyplinear_w_kernel(tc, x, weight_words, weight_scales, bias, out):
         nc.vector.memset(bigz[:, 0:1], BIG)
 
         nc.scalar.dma_start(out=brow[0:1, :], in_=bias.unsqueeze(0))
-        for h in range(2):
-            for q in range(4):
+        for q in (2, 3, 0, 1):
+            for h in range(2):
                 nc.sync.dma_start(
                     out=planes[h][32 * q : 32 * q + 16, :].bitcast(I32),
                     in_=weight_scales[4 * h : 4 * h + 4, 4 * q : 4 * q + 4, :].bitcast(I32),

@@ -76,6 +76,7 @@ def tile_hyplinear_w_kernel(tc, x, weight_words, weight_scales, bias, out):
         ds = keep.tile([P, 2], F32, name="ds")
         lv = keep.tile([P, 8], F32, name="lv")
         hh = keep.tile([P, 1], F32, name="hh")
+        hqs = keep.tile([P, 1], F32, name="hqs")
         t_sb = keep.tile([P, DOUT], F32, name="t_sb")
 
         make_identity(nc, ident[:])
@@ -235,7 +236,7 @@ def tile_hyplinear_w_kernel(tc, x, weight_words, weight_scales, bias, out):
         nc.vector.tensor_scalar(out=pb, in0=pa, scalar1=s1p[:, 6:7], scalar2=None, op0=ALU.add)
         sum_sq(7)
 
-        rnq, mmx, pqn, qg, hq = lv[:, 0:1], lv[:, 1:2], lv[:, 2:3], lv[:, 3:4], lv[:, 4:5]
+        rnq, mmx, pqn, qg = lv[:, 0:1], lv[:, 1:2], lv[:, 2:3], lv[:, 3:4]
         a1y, urg, nq = w4[:, 0:1], w4[:, 2:3], w4[:, 3:4]
         nc.vector.scalar_tensor_tensor(
             out=m2[:], in0=pb, scalar=s1p[:, NB - 1 : NB], in1=bigz[:], op0=ALU.add, op1=ALU.min
@@ -262,7 +263,7 @@ def tile_hyplinear_w_kernel(tc, x, weight_words, weight_scales, bias, out):
 
         chunks = [(0, 128, "g"), (128, 128, "s"), (256, 256, "s")]
         for j in range(1, NB - 1):
-            chunks.append((NT * j, NT, "g" if j % 2 == 0 else "s"))
+            chunks.append((NT * j, NT, "s"))
         chunks.append((NT * (NB - 1), 256, "s"))
         chunks.append((NT * (NB - 1) + 256, 256, "s"))
 
@@ -276,7 +277,7 @@ def tile_hyplinear_w_kernel(tc, x, weight_words, weight_scales, bias, out):
         def finish(c0, width, who):
             cols = slice(c0, c0 + width)
             if who == "s":
-                nc.scalar.activation(out=o_sb[:, cols], in_=t_sb[:, cols], func=ACTF.Copy, scale=hq)
+                nc.scalar.activation(out=o_sb[:, cols], in_=t_sb[:, cols], func=ACTF.Copy, scale=hqs[:])
             else:
                 nc.gpsimd.tensor_scalar(
                     out=o_sb[:, cols], in0=t_sb[:, cols], scalar1=qg, scalar2=hh[:], op0=ALU.mult, op1=ALU.mult
@@ -285,7 +286,7 @@ def tile_hyplinear_w_kernel(tc, x, weight_words, weight_scales, bias, out):
 
         for c0, width, who in chunks[:3]:
             combine(c0, width)
-        nc.vector.tensor_tensor(out=hq, in0=hh[:], in1=qg, op=ALU.mult)
+        nc.scalar.activation(out=hqs[:], in_=hh[:], func=ACTF.Copy, scale=qg)
         for c0, width, who in chunks[:3]:
             finish(c0, width, who)
         for c0, width, who in chunks[3:]:

@@ -97,13 +97,13 @@ def tile_hyplinear_w_kernel(tc, x, weight_words, weight_scales, bias, out):
         nc.vector.memset(const4[:, 3:4], -1.0)
         nc.vector.memset(bigz[:, 0:1], BIG)
 
-        nc.scalar.dma_start(out=brow[0:1, :], in_=bias.unsqueeze(0))
         for q in (2, 3, 0, 1):
             for h in range(2):
                 nc.sync.dma_start(
                     out=planes[h][32 * q : 32 * q + 16, :].bitcast(I32),
                     in_=weight_scales[4 * h : 4 * h + 4, 4 * q : 4 * q + 4, :].bitcast(I32),
                 )
+        nc.sync.dma_start(out=brow[0:1, :], in_=bias.unsqueeze(0))
         for g in range(G_FULL):
             nc.sync.dma_start(
                 out=w_full[g][:].bitcast(I32),

@@ -19,7 +19,7 @@ DOUT = 4096
 G = DIN // 512
 NT = 512
 NB = DOUT // NT
-G_FULL = 6
+G_FULL = 5
 MAXN = 0.996
 MIN_NORM = 1e-15
 CINV = 1.0 / (MAXN * MAXN)
@@ -113,12 +113,11 @@ def tile_hyplinear_w_kernel(tc, x, weight_words, weight_scales, bias, out):
         for r in range(3):
             cols = slice(4 * 1024 * r, 4 * 1024 * (r + 1))
             nc.sync.dma_start(out=w_tail[:, :, cols].bitcast(I32), in_=tail_src[:, :, cols].bitcast(I32))
-        nc.sync.dma_start(
-            out=w_tail[:, 0, 4 * 3072 :].bitcast(I32), in_=tail_src[:, 0, 4 * 3072 :].bitcast(I32)
-        )
-        for j in (6, 7):
-            cols = slice(4 * NT * j, 4 * NT * (j + 1))
-            nc.sync.dma_start(out=w_tail[:, 1, cols].bitcast(I32), in_=tail_src[:, 1, cols].bitcast(I32))
+        cols = slice(4 * NT * 6, 4 * NT * 7)
+        nc.sync.dma_start(out=w_tail[:, :, cols].bitcast(I32), in_=tail_src[:, :, cols].bitcast(I32))
+        cols = slice(4 * NT * 7, 4 * NT * 8)
+        nc.sync.dma_start(out=w_tail[:, 0:2, cols].bitcast(I32), in_=tail_src[:, 0:2, cols].bitcast(I32))
+        nc.sync.dma_start(out=w_tail[:, 2, cols].bitcast(I32), in_=tail_src[:, 2, cols].bitcast(I32))
 
         x32 = x_sb[:].bitcast(F32)
         g32 = grouped[:].bitcast(F32)
@@ -219,17 +218,17 @@ def tile_hyplinear_w_kernel(tc, x, weight_words, weight_scales, bias, out):
                 mx_pass(g, j)
         for r in range(3):
             for j in (2 * r, 2 * r + 1):
-                mx_pass(6, j)
-                mx_pass(7, j)
+                for g in range(G_FULL, G):
+                    mx_pass(g, j)
             for j in (2 * r, 2 * r + 1):
                 sum_sq(j)
                 sum_b(j)
         nc.vector.tensor_reduce(out=p05, in_=s1p[:, 0:6], axis=AX.X, op=ALU.add)
         nc.vector.tensor_scalar(out=pa, in0=p05.to_broadcast([P, 2]), scalar1=MIN_NORM, scalar2=None, op0=ALU.max)
-        mx_pass(6, 6)
-        mx_pass(6, 7)
-        mx_pass(7, 6)
-        mx_pass(7, 7)
+        for g in range(G_FULL, G):
+            mx_pass(g, 6)
+        for g in range(G_FULL, G):
+            mx_pass(g, 7)
         sum_sq(6)
         sum_b(6)
         nc.vector.tensor_reduce(out=pre2, in_=s2p[:, 0 : NB - 1], axis=AX.X, op=ALU.add)

@@ -263,8 +263,8 @@ def tile_hyplinear_w_kernel(tc, x, weight_words, weight_scales, bias, out):
         chunks = [(0, 128, "g"), (128, 128, "s"), (256, 256, "s")]
         for j in range(1, NB - 1):
             chunks.append((NT * j, NT, "s"))
-        chunks.append((NT * (NB - 1), 256, "s"))
-        chunks.append((NT * (NB - 1) + 256, 256, "s"))
+        chunks.append((NT * (NB - 1), 256, "v"))
+        chunks.append((NT * (NB - 1) + 256, 256, "v"))
 
         def combine(c0, width):
             j = c0 // NT
@@ -277,6 +277,10 @@ def tile_hyplinear_w_kernel(tc, x, weight_words, weight_scales, bias, out):
             cols = slice(c0, c0 + width)
             if who == "s":
                 nc.scalar.activation(out=o_sb[:, cols], in_=t_sb[:, cols], func=ACTF.Copy, scale=hqs[:])
+            elif who == "v":
+                nc.vector.tensor_scalar(
+                    out=o_sb[:, cols], in0=t_sb[:, cols], scalar1=qg, scalar2=hh[:], op0=ALU.mult, op1=ALU.mult
+                )
             else:
                 nc.gpsimd.tensor_scalar(
                     out=o_sb[:, cols], in0=t_sb[:, cols], scalar1=qg, scalar2=hh[:], op0=ALU.mult, op1=ALU.mult
@@ -288,6 +292,10 @@ def tile_hyplinear_w_kernel(tc, x, weight_words, weight_scales, bias, out):
         nc.scalar.activation(out=hqs[:], in_=hh[:], func=ACTF.Copy, scale=qg)
         for c0, width, who in chunks[:3]:
             finish(c0, width, who)
-        for c0, width, who in chunks[3:]:
+        for c0, width, who in chunks[3:-2]:
             combine(c0, width)
+            finish(c0, width, who)
+        for c0, width, who in chunks[-2:]:
+            combine(c0, width)
+        for c0, width, who in chunks[-2:]:
             finish(c0, width, who)

from contextlib import ExitStack

import concourse.mybir as mybir
from concourse.masks import make_identity

F32 = mybir.dt.float32
BF16 = mybir.dt.bfloat16
I32 = mybir.dt.int32
U32 = mybir.dt.uint32
U8 = mybir.dt.uint8
FP8X4 = mybir.dt.float8_e4m3fn_x4
ALU = mybir.AluOpType
ACTF = mybir.ActivationFunctionType
AX = mybir.AxisListType

P = 128
DIN = 4096
DOUT = 4096
G = DIN // 512
NT = 512
NB = DOUT // NT
G_FULL = 5
MAXN = 0.996
MIN_NORM = 1e-15
CINV = 1.0 / (MAXN * MAXN)
Z0 = 3.1063030478757594
BIG = 2.0 ** 100

FLOPS = 2 * 128 * DIN * DOUT


def tile_hyplinear_w_kernel(tc, x, weight_words, weight_scales, bias, out):
    nc = tc.nc
    with ExitStack() as ctx:
        ctx.enter_context(tc.manual_schedule())
        keep = ctx.enter_context(tc.tile_pool(name="keep", bufs=1))
        work = ctx.enter_context(tc.tile_pool(name="work", bufs=3))
        psum = ctx.enter_context(tc.psum_pool(name="psum", bufs=1))

        x_sb = keep.tile([P, DIN], BF16, name="x_sb", align_bytes=64)
        grouped = keep.tile([P, G, P, 4], BF16, name="grouped", align_bytes=64)
        xq = keep.tile([P, G * P], U32, name="xq", align_bytes=64)
        xs = keep.tile([P, G * P], U8, name="xs", align_bytes=64)
        planes = [keep.tile([P, DOUT], U8, name="planes%d" % h, align_bytes=64) for h in range(2)]
        w_full = [keep.tile([P, 4 * DOUT], U8, name="w%d" % g, align_bytes=64) for g in range(G_FULL)]
        w_tail = keep.tile([P, G - G_FULL, 4 * DOUT], U8, name="w_tail", align_bytes=64)
        brow = keep.tile([P, DOUT], BF16, name="brow")
        b_bc = keep.tile([P, DOUT], BF16, name="b_bc")
        junkbig = keep.tile([P, DOUT], BF16, name="junkbig")
        o_sb = keep.tile([P, DOUT], F32, name="o_sb")
        ones = keep.tile([P, P], BF16, name="ones")
        ident = keep.tile([P, P], F32, name="ident")
        e4 = keep.tile([P, 4], F32, name="e4")
        em = keep.tile([P, 2], F32, name="em")

        sxb = keep.tile([P, 2], F32, name="sxb")
        n4 = keep.tile([P, 4], F32, name="n4")
        pw4 = keep.tile([P, 4], F32, name="pw4")
        ev = keep.tile([P, 16], F32, name="ev")
        ll = keep.tile([P, 2], F32, name="ll")
        tb = keep.tile([P, 1], F32, name="tb")
        s1p = keep.tile([P, NB], F32, name="s1p")
        s2p = keep.tile([P, NB], F32, name="s2p")
        onec = keep.tile([P, 1], F32, name="onec")
        ex2 = keep.tile([P, 2], F32, name="ex2")
        const4 = keep.tile([P, 4], F32, name="const4")
        k2 = keep.tile([P, 2], F32, name="k2")
        g2p = keep.tile([P, 2], F32, name="g2p")
        pc = keep.tile([P, 3], F32, name="pc")
        bigz = keep.tile([P, 2], F32, name="bigz")
        pab = keep.tile([P, 8], F32, name="pab")
        m2 = keep.tile([P, 2], F32, name="m2")
        pw2 = keep.tile([P, 2], F32, name="pw2")
        coef4 = keep.tile([P, 4], F32, name="coef4")
        w4 = keep.tile([P, 4], F32, name="lvl1")
        ds = keep.tile([P, 2], F32, name="ds")
        lv = keep.tile([P, 8], F32, name="lv")
        hh = keep.tile([P, 1], F32, name="hh")
        hqs = keep.tile([P, 1], F32, name="hqs")
        t_sb = keep.tile([P, DOUT], F32, name="t_sb")

        make_identity(nc, ident[:])
        nc.sync.dma_start(out=x_sb[:], in_=x)
        for h in range(2):
            nc.vector.memset(planes[h][:].bitcast(I32), 0)
        nc.vector.memset(brow[:].bitcast(I32), 0)
        nc.vector.memset(ones[:], 1.0)
        nc.vector.memset(e4[:, 0:1], 0.5)
        nc.vector.memset(e4[:, 1:2], -0.5)
        nc.vector.memset(e4[:, 2:3], 0.5)
        nc.vector.memset(e4[:, 3:4], -0.5)
        nc.vector.memset(em[:], -0.5)
        nc.vector.memset(onec[:], 1.0)
        nc.vector.memset(ex2[:, 0:1], -0.5)
        nc.vector.memset(ex2[:, 1:2], 0.5)
        nc.vector.memset(const4[:, 2:3], 0.0)
        nc.vector.memset(const4[:, 3:4], -1.0)
        nc.vector.memset(bigz[:, 0:1], BIG)

        for q in (2, 3, 0, 1):
            for h in range(2):
                nc.sync.dma_start(
                    out=planes[h][32 * q : 32 * q + 16, :].bitcast(I32),
                    in_=weight_scales[4 * h : 4 * h + 4, 4 * q : 4 * q + 4, :].bitcast(I32),
                )
        nc.sync.dma_start(out=brow[0:1, :], in_=bias.unsqueeze(0))
        for g in range(G_FULL):
            nc.sync.dma_start(
                out=w_full[g][:].bitcast(I32),
                in_=weight_words[g].rearrange("p n t -> p (n t)").bitcast(I32),
            )
        tail_src = weight_words[G_FULL:G].rearrange("g p n t -> p g (n t)")
        for r in range(3):
            cols = slice(4 * 1024 * r, 4 * 1024 * (r + 1))
            nc.sync.dma_start(out=w_tail[:, :, cols].bitcast(I32), in_=tail_src[:, :, cols].bitcast(I32))
        cols = slice(4 * NT * 6, 4 * NT * 7)
        nc.sync.dma_start(out=w_tail[:, :, cols].bitcast(I32), in_=tail_src[:, :, cols].bitcast(I32))
        cols = slice(4 * NT * 7, 4 * NT * 8)
        nc.sync.dma_start(out=w_tail[:, 0:2, cols].bitcast(I32), in_=tail_src[:, 0:2, cols].bitcast(I32))
        nc.sync.dma_start(out=w_tail[:, 2, cols].bitcast(I32), in_=tail_src[:, 2, cols].bitcast(I32))

        x32 = x_sb[:].bitcast(F32)
        g32 = grouped[:].bitcast(F32)
        xts = []
        for k in range(4):
            xt = psum.tile([P, 2, 2, P], F32, name="xt%d" % k, tag="bank%d" % k)
            xts.append(xt)
            for gi in range(2):
                g = 2 * k + gi
                for u in range(2):
                    nc.tensor.transpose(xt[:, gi, u, :], x32[:, 256 * g + u : 256 * (g + 1) : 2], ident[:])
        for k in range(4):
            src = xts[k][:].rearrange("p g u m -> p g m u")
            dst = g32[:, 2 * k : 2 * k + 2, :, :]
            if k % 2 == 0:
                nc.vector.tensor_copy(out=dst, in_=src)
            else:
                nc.scalar.copy(out=dst, in_=src)
        for h in range(2):
            nc.vector.quantize_mx(
                out=xq[:, 512 * h : 512 * (h + 1)].bitcast(FP8X4),
                scales=xs[:, 512 * h : 512 * (h + 1)],
                in_=grouped[:, 4 * h : 4 * h + 4, :, :].rearrange("p g m t -> p (g m t)"),
            )

        for k in range(4):
            bb = psum.tile([P, 2 * NT], BF16, name="bb%d" % k, tag="bank%d" % (4 + k))
            for i in range(2):
                c0 = 2 * NT * k + NT * i
                nc.tensor.matmul(
                    bb[:, NT * i : NT * (i + 1)], lhsT=ones[:], rhs=brow[:, c0 : c0 + NT], start=True, stop=True
                )
            dst = b_bc[:, 2 * NT * k : 2 * NT * (k + 1)]
            if k % 2 == 0:
                nc.scalar.copy(out=dst, in_=bb[:])
            else:
                nc.vector.tensor_copy(out=dst, in_=bb[:])

        nc.scalar.activation(out=junkbig[:], in_=x_sb[:], func=ACTF.Square, accum_out=sxb[:, 0:1])
        nc.scalar.activation(out=junkbig[:], in_=b_bc[:], func=ACTF.Square, accum_out=sxb[:, 1:2])
        for i in range(2):
            nc.vector.tensor_scalar(
                out=n4[:, 2 * i : 2 * i + 2], in0=sxb[:, i : i + 1].to_broadcast([P, 2]),
                scalar1=MIN_NORM, scalar2=None, op0=ALU.max,
            )
        nc.gpsimd.tensor_tensor(out=pw4[:], in0=n4[:], in1=e4[:], op=ALU.pow)
        um, up, dl, cc, gam, rcc = ev[:, 0:1], ev[:, 1:3], ev[:, 3:4], ev[:, 4:5], ev[:, 5:6], ev[:, 6:7]
        y2 = k2[:, 0:1]
        nc.vector.tensor_scalar(out=um, in0=pw4[:, 0:1], scalar1=1.0 - 1e-5, scalar2=None, op0=ALU.min)
        nc.vector.tensor_scalar(out=up[:, 0:1], in0=um, scalar1=1.0, scalar2=None, op0=ALU.add)
        nc.vector.tensor_scalar(out=up[:, 1:2], in0=um, scalar1=-1.0, scalar2=1.0, op0=ALU.mult, op1=ALU.add)
        nc.scalar.activation(out=ll[:], in_=up, func=ACTF.Ln)
        nc.scalar.activation(out=tb[:], in_=pw4[:, 2:3], func=ACTF.Tanh)
        nc.vector.tensor_tensor(out=dl, in0=ll[:, 0:1], in1=ll[:, 1:2], op=ALU.subtract)
        nc.vector.tensor_scalar(out=cc, in0=dl, scalar1=pw4[:, 1:2], scalar2=0.5, op0=ALU.mult, op1=ALU.mult)
        nc.vector.tensor_scalar(out=gam, in0=tb[:], scalar1=MAXN, scalar2=pw4[:, 3:4], op0=ALU.min, op1=ALU.mult)
        nc.vector.tensor_scalar(out=y2, in0=gam, scalar1=gam, scalar2=sxb[:, 1:2], op0=ALU.mult, op1=ALU.mult)
        nc.vector.tensor_scalar(out=k2[:, 1:2], in0=onec[:], scalar1=CINV, scalar2=None, op0=ALU.mult)
        nc.vector.tensor_scalar(out=const4[:, 0:1], in0=y2, scalar1=1.0, scalar2=None, op0=ALU.add)
        nc.vector.tensor_scalar(out=const4[:, 1:2], in0=y2, scalar1=1.0, scalar2=CINV, op0=ALU.add, op1=ALU.mult)
        nc.vector.tensor_scalar(out=g2p[:, 0:1], in0=gam, scalar1=2.0, scalar2=None, op0=ALU.mult)
        nc.vector.tensor_scalar(out=g2p[:, 1:2], in0=gam, scalar1=2.0 * CINV, scalar2=None, op0=ALU.mult)
        nc.vector.reciprocal(out=pc[:, 2:3], in_=gam)
        nc.vector.reciprocal(out=rcc, in_=cc)
        nc.vector.tensor_scalar(out=bigz[:, 1:2], in0=rcc, scalar1=rcc, scalar2=Z0 * Z0, op0=ALU.mult, op1=ALU.mult)

        acc = [psum.tile([P, NT], F32, name="acc%d" % j, tag="bank%d" % j) for j in range(NB)]

        def mx_pass(g, j):
            if g < G_FULL:
                words = w_full[g][:, 4 * NT * j : 4 * NT * (j + 1)]
            else:
                words = w_tail[:, g - G_FULL, 4 * NT * j : 4 * NT * (j + 1)]
            nc.tensor.matmul_mx(
                out=acc[j][:],
                lhsT=xq[:, P * g : P * (g + 1)].bitcast(FP8X4),
                lhsT_scale=xs[:, P * g : P * (g + 1)],
                rhs=words.bitcast(FP8X4),
                rhs_scale=planes[g // 4][4 * (g % 4) : P, NT * j : NT * (j + 1)],
                start=(g == 0),
                stop=(g == G - 1),
            )

        def sum_sq(j):
            junk = work.tile([P, NT], F32, name="junk", tag="junk")
            nc.scalar.activation(out=junk[:], in_=acc[j][:], func=ACTF.Square, accum_out=s1p[:, j : j + 1])

        def sum_b(j):
            junk = work.tile([P, NT], F32, name="junkv", tag="junkv")
            nc.vector.scalar_tensor_tensor(
                out=junk[:], in0=acc[j][:], scalar=1.0, in1=b_bc[:, NT * j : NT * (j + 1)],
                op0=ALU.mult, op1=ALU.mult, accum_out=s2p[:, j : j + 1],
            )

        p05, pa, pb, pre2 = pab[:, 0:1], pab[:, 1:3], pab[:, 3:5], pab[:, 5:6]
        for g in range(G_FULL):
            for j in range(NB):
                mx_pass(g, j)
        for r in range(3):
            for j in (2 * r, 2 * r + 1):
                for g in range(G_FULL, G):
                    mx_pass(g, j)
            for j in (2 * r, 2 * r + 1):
                sum_sq(j)
                sum_b(j)
        nc.vector.tensor_reduce(out=p05, in_=s1p[:, 0:6], axis=AX.X, op=ALU.add)
        nc.vector.tensor_scalar(out=pa, in0=p05.to_broadcast([P, 2]), scalar1=MIN_NORM, scalar2=None, op0=ALU.max)
        for g in range(G_FULL, G):
            mx_pass(g, 6)
        for g in range(G_FULL, G):
            mx_pass(g, 7)
        sum_sq(6)
        sum_b(6)
        nc.vector.tensor_reduce(out=pre2, in_=s2p[:, 0 : NB - 1], axis=AX.X, op=ALU.add)
        nc.vector.tensor_scalar(out=pb, in0=pa, scalar1=s1p[:, 6:7], scalar2=None, op0=ALU.add)
        sum_sq(7)

        rnq, mmx, pqn, qg = lv[:, 0:1], lv[:, 1:2], lv[:, 2:3], lv[:, 3:4]
        a1y, urg, nq = w4[:, 0:1], w4[:, 2:3], w4[:, 3:4]
        nc.vector.scalar_tensor_tensor(
            out=m2[:], in0=pb, scalar=s1p[:, NB - 1 : NB], in1=bigz[:], op0=ALU.add, op1=ALU.min
        )
        sum_b(7)
        nc.gpsimd.tensor_tensor(out=pw2[:], in0=m2[:], in1=ex2[:], op=ALU.pow)
        nc.vector.scalar_tensor_tensor(
            out=pc[:, 0:2], in0=s2p[:, NB - 1 : NB].to_broadcast([P, 2]), scalar=pre2, in1=g2p[:],
            op0=ALU.add, op1=ALU.mult,
        )
        nc.scalar.activation(out=coef4[:, 3:4], in_=pw2[:, 1:2], func=ACTF.Tanh, scale=cc)
        nc.vector.tensor_scalar(out=coef4[:, 0:3], in0=pc[:], scalar1=pw2[:, 0:1], scalar2=None, op0=ALU.mult)
        nc.vector.scalar_tensor_tensor(
            out=w4[:], in0=coef4[:], scalar=coef4[:, 3:4], in1=const4[:], op0=ALU.mult, op1=ALU.add
        )
        nc.vector.scalar_tensor_tensor(out=ds[:], in0=k2[:], scalar=nq, in1=w4[:, 0:2], op0=ALU.mult, op1=ALU.add)
        nc.vector.reciprocal(out=rnq, in_=nq)
        nc.vector.scalar_tensor_tensor(
            out=mmx, in0=ds[:, 1:2], scalar=ds[:, 0:1], in1=ds[:, 0:1], op0=ALU.max, op1=ALU.mult
        )
        nc.gpsimd.tensor_tensor(out=hh[:], in0=mmx, in1=em[:, 0:1], op=ALU.pow)
        nc.vector.scalar_tensor_tensor(out=pqn, in0=a1y, scalar=urg, in1=rnq, op0=ALU.mult, op1=ALU.mult)
        nc.vector.tensor_tensor(out=qg, in0=nq, in1=gam, op=ALU.mult)

        chunks = [(0, 128, "g"), (128, 128, "s"), (256, 256, "s")]
        for j in range(1, NB - 1):
            chunks.append((NT * j, NT, "s"))
        chunks.append((NT * (NB - 1), 256, "v"))
        chunks.append((NT * (NB - 1) + 256, 256, "v"))

        def combine(c0, width):
            j = c0 // NT
            nc.vector.scalar_tensor_tensor(
                out=t_sb[:, c0 : c0 + width], in0=acc[j][:, c0 - NT * j : c0 - NT * j + width], scalar=pqn,
                in1=b_bc[:, c0 : c0 + width], op0=ALU.mult, op1=ALU.subtract,
            )

        def finish(c0, width, who):
            cols = slice(c0, c0 + width)
            if who == "s":
                nc.scalar.activation(out=o_sb[:, cols], in_=t_sb[:, cols], func=ACTF.Copy, scale=hqs[:])
            elif who == "v":
                nc.vector.tensor_scalar(
                    out=o_sb[:, cols], in0=t_sb[:, cols], scalar1=qg, scalar2=hh[:], op0=ALU.mult, op1=ALU.mult
                )
            else:
                nc.gpsimd.tensor_scalar(
                    out=o_sb[:, cols], in0=t_sb[:, cols], scalar1=qg, scalar2=hh[:], op0=ALU.mult, op1=ALU.mult
                )
            nc.sync.dma_start(out=out[:, cols], in_=o_sb[:, cols])

        for c0, width, who in chunks[:3]:
            combine(c0, width)
        nc.scalar.activation(out=hqs[:], in_=hh[:], func=ACTF.Copy, scale=qg)
        for c0, width, who in chunks[:3]:
            finish(c0, width, who)
        for c0, width, who in chunks[3:-2]:
            combine(c0, width)
            finish(c0, width, who)
        for c0, width, who in chunks[-2:]:
            combine(c0, width)
        for c0, width, who in chunks[-2:]:
            finish(c0, width, who)
